import numpy as np
import ml_dtypes


def mxq(x, axis, fmt="e4m3"):
    dtype, down = {"e4m3": (ml_dtypes.float8_e4m3fn, 7), "e5m2": (ml_dtypes.float8_e5m2, 14)}[fmt]
    v = np.moveaxis(np.asarray(x, np.float32).astype(ml_dtypes.bfloat16).astype(np.float64), axis, -1)
    blocks = v.reshape(v.shape[:-1] + (-1, 32))
    amax = np.abs(blocks).max(-1, keepdims=True)
    byte = np.maximum(np.where(amax > 0, np.frexp(amax)[1] - 1 + 127, 0) - down, 1)
    scale = np.exp2(byte - 127.0)
    codes = (blocks / scale).astype(np.float32).astype(dtype).astype(np.float64)
    return np.moveaxis((codes * scale).reshape(v.shape), -1, axis)


WIDE = False


def mx_kscale(k):
    if not WIDE:
        return np.ones(k)
    levels = np.array([10, -10, 5, -5, 0])
    a = np.random.permutation(np.resize(levels, k // 512 * 4)).reshape(k // 512, 4)
    idx = np.arange(k)
    return np.exp2(a[idx // 512, idx % 128 // 32])


BF16 = ml_dtypes.bfloat16


def bf(x):
    return np.asarray(x, np.float32).astype(BF16)


def f64(x):
    return np.asarray(x).astype(np.float64)


B, DA, DB, DC, OUT, NS = 256, 1024, 512, 2048, 1024, 3
EPS = 1e-5
STREAMS = (("a", DA), ("b", DB), ("c", DC))


def layer_norm(x, w, b):
    mu = x.mean(-1, keepdims=True)
    var = np.square(x - mu).mean(-1, keepdims=True)
    return (x - mu) / np.sqrt(var + EPS) * w + b


def setup_inputs():
    inp = {}
    for name, d in STREAMS:
        t = mx_kscale(d)
        loud = np.exp2(-np.random.uniform(0.0, 8.0, (B, 1)))
        inp["x_" + name] = bf((np.random.standard_normal((B, d)) + 0.5 * np.random.standard_normal((B, 1))) * loud)
        inp["ln_w_" + name] = bf((1.0 + 0.1 * np.random.standard_normal(d)) * t)
        inp["ln_b_" + name] = bf(0.1 * np.random.standard_normal(d) * t)
        inp["W_" + name] = bf(np.random.standard_normal((d, OUT)) / np.sqrt(d) / t[:, None])
        inp["b_" + name] = bf(0.2 * np.random.standard_normal(OUT))
        inp["Wg_" + name] = bf(np.random.standard_normal((d, NS * OUT)) / np.sqrt(d) / t[:, None])
        inp["bg_" + name] = bf(0.2 * np.random.standard_normal(NS * OUT))
    return inp


def reference(x_a, ln_w_a, ln_b_a, W_a, b_a, Wg_a, bg_a,
              x_b, ln_w_b, ln_b_b, W_b, b_b, Wg_b, bg_b,
              x_c, ln_w_c, ln_b_c, W_c, b_c, Wg_c, bg_c):
    streams = ((x_a, ln_w_a, ln_b_a, W_a, b_a, Wg_a, bg_a),
               (x_b, ln_w_b, ln_b_b, W_b, b_b, Wg_b, bg_b),
               (x_c, ln_w_c, ln_b_c, W_c, b_c, Wg_c, bg_c))
    gate_logits = 0.0
    outputs = []
    for x, lw, lb, W, b, Wg, bg in streams:
        f = np.maximum(layer_norm(f64(x), f64(lw), f64(lb)), 0.0)
        fq = mxq(f, 1, "e4m3")
        outputs.append((fq @ mxq(f64(W), 0, "e4m3")) + f64(b))
        gate_logits = gate_logits + ((fq @ mxq(f64(Wg), 0, "e4m3")) + f64(bg))
    g = gate_logits.reshape(B, NS, OUT)
    e = np.exp(g - g.max(1, keepdims=True))
    gate = e / e.sum(1, keepdims=True)
    return sum(gate[:, i] * outputs[i] for i in range(NS))

@@ -1,0 +1,325 @@
+from contextlib import ExitStack
+
+import concourse.mybir as mybir
+from concourse.masks import make_identity
+
+F32 = mybir.dt.float32
+BF16 = mybir.dt.bfloat16
+U32 = mybir.dt.uint32
+U8 = mybir.dt.uint8
+FP8X4 = mybir.dt.float8_e4m3fn_x4
+ACT = mybir.ActivationFunctionType
+ALU = mybir.AluOpType
+
+P = 128
+PACK = 4
+K_PASS = P * PACK
+ROWS = 256
+ROW_TILES = ROWS // P
+OUT = 1024
+GATES = 3
+WIDTHS = (1024, 512, 2048)
+EPS = 1e-5
+BLOCK = 512
+BLOCKS = OUT // BLOCK
+COL_TILES = BLOCK // P
+PAIRS = COL_TILES // 2
+VECTOR_SHARE_16THS = 8
+BN_CHUNK = 512
+QUANTISE_WORDS = 1024
+
+PASSES = tuple((n, c) for n in range(3) for c in range(WIDTHS[n] // K_PASS))
+K_TILES = sum(WIDTHS) // P
+
+FLOPS = 2 * ROWS * sum(WIDTHS) * (OUT + GATES * OUT)
+
+
+def tile_vectormerge_pa_kernel(
+    tc,
+    x_a, ln_w_a, ln_b_a, W_a, b_a, Wg_a, bg_a,
+    x_b, ln_w_b, ln_b_b, W_b, b_b, Wg_b, bg_b,
+    x_c, ln_w_c, ln_b_c, W_c, b_c, Wg_c, bg_c,
+    out,
+):
+    nc = tc.nc
+    xs = (x_a, x_b, x_c)
+    ln_ws = (ln_w_a, ln_w_b, ln_w_c)
+    ln_bs = (ln_b_a, ln_b_b, ln_b_c)
+    Ws = (W_a, W_b, W_c)
+    bs = (b_a, b_b, b_c)
+    Wgs = (Wg_a, Wg_b, Wg_c)
+    bgs = (bg_a, bg_b, bg_c)
+    B_ROWS = OUT // P
+    BG_ROWS = GATES * B_ROWS
+
+    with ExitStack() as stack:
+        const = stack.enter_context(tc.tile_pool(name="const", bufs=1))
+        raw_pool = stack.enter_context(tc.tile_pool(name="raw", bufs=3))
+        grouped_pool = stack.enter_context(tc.tile_pool(name="grouped", bufs=2))
+        codes_pool = stack.enter_context(tc.tile_pool(name="codes", bufs=len(PASSES)))
+        acc_pool = stack.enter_context(tc.psum_pool(name="acc", bufs=6))
+        turn_pool = stack.enter_context(tc.psum_pool(name="turn", bufs=2))
+
+        ident = const.tile([P, P], F32)
+        make_identity(nc, ident[:])
+        x_sb = []
+        for n in range(3):
+            x_n = const.tile([P, ROW_TILES, WIDTHS[n]], BF16, name="x%d" % n)
+            nc.gpsimd.dma_start(out=x_n[:], in_=xs[n].rearrange("(m p) d -> p m d", p=P))
+            x_sb.append(x_n)
+        minus_half = const.tile([P, ROW_TILES], F32)
+        nc.vector.memset(minus_half[:], -0.5)
+        f_codes = const.tile([P, len(PASSES), ROWS], U32, align_bytes=64)
+        f_scales = const.tile([P, len(PASSES), ROWS], U8, align_bytes=64)
+
+        ln_rows = const.tile([P, P], BF16)
+        bias_rows = const.tile([P, P], BF16)
+        nc.vector.memset(ln_rows[:], 0.0)
+        nc.vector.memset(bias_rows[:], 0.0)
+        k_tile0 = 0
+        for n in range(3):
+            k_tiles = WIDTHS[n] // P
+            nc.sync.dma_start(
+                out=ln_rows[k_tile0 : k_tile0 + k_tiles, :],
+                in_=ln_ws[n].rearrange("(r c) -> r c", c=P),
+            )
+            nc.sync.dma_start(
+                out=ln_rows[K_TILES + k_tile0 : K_TILES + k_tile0 + k_tiles, :],
+                in_=ln_bs[n].rearrange("(r c) -> r c", c=P),
+            )
+            k_tile0 += k_tiles
+        for n in range(3):
+            nc.gpsimd.dma_start(
+                out=bias_rows[n * B_ROWS : (n + 1) * B_ROWS, :],
+                in_=bs[n].rearrange("(r c) -> r c", c=P),
+            )
+            nc.gpsimd.dma_start(
+                out=bias_rows[3 * B_ROWS + n * BG_ROWS : 3 * B_ROWS + (n + 1) * BG_ROWS, :],
+                in_=bgs[n].rearrange("(r c) -> r c", c=P),
+            )
+
+        def to_columns(rows_bf16, name):
+            rows_f32 = const.tile([P, P], F32, name=name + "_f32")
+            nc.vector.tensor_copy(out=rows_f32[:], in_=rows_bf16[:])
+            turned = turn_pool.tile([P, BLOCK], F32, tag="turn", name=name + "_ps")
+            nc.tensor.transpose(turned[:, 0:P], rows_f32[:], ident[:])
+            columns = const.tile([P, P], F32, name=name + "_cols")
+            nc.vector.tensor_copy(out=columns[:], in_=turned[:, 0:P])
+            return columns
+
+        ln_cols = to_columns(ln_rows, "ln")
+        bias_cols = to_columns(bias_rows, "bias")
+        bg_sum = const.tile([P, BG_ROWS], F32)
+        bg0 = 3 * B_ROWS
+        nc.vector.tensor_tensor(
+            out=bg_sum[:], in0=bias_cols[:, bg0 : bg0 + BG_ROWS],
+            in1=bias_cols[:, bg0 + BG_ROWS : bg0 + 2 * BG_ROWS], op=ALU.add,
+        )
+        nc.vector.tensor_tensor(
+            out=bg_sum[:], in0=bg_sum[:],
+            in1=bias_cols[:, bg0 + 2 * BG_ROWS : bg0 + 3 * BG_ROWS], op=ALU.add,
+        )
+
+        with tc.tile_pool(name="norm", bufs=2) as norm:
+            q = 0
+            for n in range(3):
+                d = WIDTHS[n]
+                chunks = d // BN_CHUNK
+                stats = norm.tile([P, ROW_TILES, chunks, 6], F32, name="stats%d" % n, bufs=1)
+                mean_var = norm.tile([P, ROW_TILES, 2], F32, tag="mean_var")
+                for m in range(ROW_TILES):
+                    for j in range(chunks):
+                        nc.vector.bn_stats(
+                            out=stats[:, m, j, :],
+                            in_=x_sb[n][:, m, j * BN_CHUNK : (j + 1) * BN_CHUNK],
+                        )
+                    nc.vector.bn_aggr(
+                        out=mean_var[:, m, :], in_=stats[:, m, :, :].rearrange("p c s -> p (c s)")
+                    )
+                var_eps = norm.tile([P, ROW_TILES], F32, tag="var_eps")
+                nc.vector.tensor_scalar_add(out=var_eps[:], in0=mean_var[:, :, 1], scalar1=EPS)
+                rstd = norm.tile([P, ROW_TILES], F32, tag="rstd")
+                nc.gpsimd.tensor_tensor(out=rstd[:], in0=var_eps[:], in1=minus_half[:], op=ALU.pow)
+                shift = norm.tile([P, ROW_TILES], F32, tag="shift")
+                nc.vector.scalar_tensor_tensor(
+                    out=shift[:], in0=mean_var[:, :, 0], scalar=-1.0, in1=rstd[:],
+                    op0=ALU.mult, op1=ALU.mult,
+                )
+                for c in range(d // K_PASS):
+                    z = []
+                    for m in range(ROW_TILES):
+                        z_m = norm.tile([P, K_PASS], F32, tag="z", bufs=4, name="z%d" % m)
+                        nc.scalar.activation(
+                            out=z_m[:], in_=x_sb[n][:, m, c * K_PASS : (c + 1) * K_PASS],
+                            func=ACT.Identity, bias=shift[:, m : m + 1], scale=rstd[:, m : m + 1],
+                        )
+                        z.append(z_m)
+                    f_t = norm.tile([P, PACK, ROWS], BF16, tag="f_t")
+                    for half in range(PACK // 2):
+                        z_turned = turn_pool.tile([P, 2, ROWS], F32, tag="turn")
+                        for u in range(2):
+                            t = 2 * half + u
+                            for m in range(ROW_TILES):
+                                nc.tensor.transpose(
+                                    z_turned[:, u, m * P : (m + 1) * P],
+                                    z[m][:, t * P : (t + 1) * P],
+                                    ident[:],
+                                )
+                        for u in range(2):
+                            t = 2 * half + u
+                            kt = PACK * q + t
+                            nc.scalar.activation(
+                                out=f_t[:, t, :], in_=z_turned[:, u, :], func=ACT.Relu,
+                                bias=ln_cols[:, K_TILES + kt : K_TILES + kt + 1],
+                                scale=ln_cols[:, kt : kt + 1],
+                            )
+                    f_grouped = norm.tile([P, ROWS, PACK], BF16, tag="f_grouped", align_bytes=64)
+                    nc.vector.tensor_copy(out=f_grouped[:], in_=f_t[:].rearrange("p t r -> p r t"))
+                    nc.vector.quantize_mx(
+                        out=f_codes[:, q, :].bitcast(FP8X4),
+                        scales=f_scales[:, q, :],
+                        in_=f_grouped[:].rearrange("p r t -> p (r t)"),
+                    )
+                    q += 1
+
+        def quantise_weights(pieces, kind, bufs):
+            width = len(pieces) * BLOCK
+            raw = raw_pool.tile([P, PACK, width], BF16, tag="raw_" + kind)
+            for i, piece in enumerate(pieces):
+                nc.sync.dma_start(
+                    out=raw[:, :, i * BLOCK : (i + 1) * BLOCK],
+                    in_=piece.rearrange("(t p) w -> p t w", p=P),
+                )
+            grouped = grouped_pool.tile([P, width, PACK], BF16, tag="grouped_" + kind, align_bytes=64)
+            dst = grouped[:].rearrange("p (c i) t -> p c t i", i=4)
+            src = raw[:].rearrange("p t (c i) -> p c t i", i=4)
+            split = width * VECTOR_SHARE_16THS // 16 // 4
+            nc.vector.tensor_copy(out=dst[:, 0:split], in_=src[:, 0:split])
+            nc.scalar.copy(out=dst[:, split:], in_=src[:, split:])
+            codes = codes_pool.tile([P, width], U32, tag="codes_" + kind, align_bytes=64, bufs=bufs)
+            scales = codes_pool.tile([P, width], U8, tag="scales_" + kind, align_bytes=64, bufs=bufs)
+            for col0 in range(0, width, QUANTISE_WORDS):
+                cols = min(QUANTISE_WORDS, width - col0)
+                nc.vector.quantize_mx(
+                    out=codes[:, col0 : col0 + cols].bitcast(FP8X4),
+                    scales=scales[:, col0 : col0 + cols],
+                    in_=grouped[:, col0 : col0 + cols, :].rearrange("p w t -> p (w t)"),
+                )
+            return codes, scales
+
+        def product(acc, weights, col0, passes):
+            for i, qq in enumerate(passes):
+                codes, scales = weights[qq]
+                nc.tensor.matmul_mx(
+                    out=acc,
+                    lhsT=codes[:, col0 : col0 + P].bitcast(FP8X4),
+                    lhsT_scale=scales[:, col0 : col0 + P],
+                    rhs=f_codes[:, qq, :].bitcast(FP8X4),
+                    rhs_scale=f_scales[:, qq, :],
+                    start=(i == 0),
+                    stop=(i == len(passes) - 1),
+                )
+
+        all_passes = list(range(len(PASSES)))
+        with tc.tile_pool(name="merge", bufs=2) as merge:
+            for h in range(BLOCKS):
+                gate_weights = []
+                for n, c in PASSES:
+                    k_rows = slice(c * K_PASS, (c + 1) * K_PASS)
+                    gate_weights.append(quantise_weights(
+                        [Wgs[n][k_rows, i * OUT + h * BLOCK : i * OUT + (h + 1) * BLOCK] for i in range(GATES)],
+                        "gates", len(PASSES) + 2,
+                    ))
+
+                denom_turned = [
+                    turn_pool.tile([P, BLOCK], F32, tag="turn", name="denom_turned%d" % m)
+                    for m in range(ROW_TILES)
+                ]
+                e_tiles = []
+                for pair in range(PAIRS):
+                    logits = [acc_pool.tile([P, 2, ROWS], F32, tag="acc", name="logits%d" % i) for i in range(GATES)]
+                    for u in range(2):
+                        for i in range(GATES):
+                            product(logits[i][:, u, :], gate_weights, i * BLOCK + (2 * pair + u) * P, all_passes)
+                    for u in range(2):
+                        ct = 2 * pair + u
+                        j = h * COL_TILES + ct
+                        bg = [bg_sum[:, B_ROWS * i + j : B_ROWS * i + j + 1] for i in range(GATES)]
+                        l0 = merge.tile([P, ROWS], F32, tag="l0")
+                        nc.scalar.activation(out=l0[:], in_=logits[0][:, u, :], func=ACT.Identity, bias=bg[0])
+                        top01 = merge.tile([P, ROWS], F32, tag="top01")
+                        nc.vector.scalar_tensor_tensor(
+                            out=top01[:], in0=logits[1][:, u, :], scalar=bg[1], in1=l0[:],
+                            op0=ALU.add, op1=ALU.max,
+                        )
+                        top = merge.tile([P, ROWS], F32, tag="top")
+                        nc.vector.scalar_tensor_tensor(
+                            out=top[:], in0=logits[2][:, u, :], scalar=bg[2], in1=top01[:],
+                            op0=ALU.add, op1=ALU.max,
+                        )
+                        e = merge.tile([P, GATES, ROWS], F32, tag="e", bufs=COL_TILES)
+                        nc.vector.tensor_tensor(out=e[:, 0, :], in0=l0[:], in1=top[:], op=ALU.subtract)
+                        for i in (1, 2):
+                            nc.vector.scalar_tensor_tensor(
+                                out=e[:, i, :], in0=logits[i][:, u, :], scalar=bg[i], in1=top[:],
+                                op0=ALU.add, op1=ALU.subtract,
+                            )
+                        nc.scalar.activation(out=e[:], in_=e[:], func=ACT.Exp)
+                        e_tiles.append(e)
+                        for m in range(ROW_TILES):
+                            for i in range(GATES):
+                                nc.tensor.matmul(
+                                    out=denom_turned[m][:, ct * P : (ct + 1) * P],
+                                    lhsT=e[:, i, m * P : (m + 1) * P],
+                                    rhs=ident[:],
+                                    start=(i == 0),
+                                    stop=(i == GATES - 1),
+                                )
+                recip = merge.tile([P, ROW_TILES, BLOCK], F32, tag="recip", bufs=1)
+                for m in range(ROW_TILES):
+                    nc.scalar.activation(out=recip[:, m, :], in_=denom_turned[m][:], func=ACT.Ln)
+                nc.scalar.activation(out=recip[:], in_=recip[:], func=ACT.Exp, scale=-1.0)
+
+                numer = merge.tile([P, COL_TILES, ROWS], F32, tag="numer", bufs=1)
+                for n in range(3):
+                    own_passes = [qq for qq in all_passes if PASSES[qq][0] == n]
+                    value_weights = {}
+                    for qq in own_passes:
+                        c = PASSES[qq][1]
+                        value_weights[qq] = quantise_weights(
+                            [Ws[n][c * K_PASS : (c + 1) * K_PASS, h * BLOCK : (h + 1) * BLOCK]], "values", len(PASSES)
+                        )
+                    for pair in range(PAIRS):
+                        y = acc_pool.tile([P, 2, ROWS], F32, tag="acc")
+                        for u in range(2):
+                            product(y[:, u, :], value_weights, (2 * pair + u) * P, own_passes)
+                        for u in range(2):
+                            ct = 2 * pair + u
+                            j = h * COL_TILES + ct
+                            b_col = bias_cols[:, B_ROWS * n + j : B_ROWS * n + j + 1]
+                            if n == 0:
+                                nc.vector.scalar_tensor_tensor(
+                                    out=numer[:, ct, :], in0=y[:, u, :], scalar=b_col, in1=e_tiles[ct][:, n, :],
+                                    op0=ALU.add, op1=ALU.mult,
+                                )
+                            else:
+                                ey = merge.tile([P, ROWS], F32, tag="ey")
+                                nc.vector.scalar_tensor_tensor(
+                                    out=ey[:], in0=y[:, u, :], scalar=b_col, in1=e_tiles[ct][:, n, :],
+                                    op0=ALU.add, op1=ALU.mult,
+                                )
+                                nc.vector.tensor_tensor(
+                                    out=numer[:, ct, :], in0=numer[:, ct, :], in1=ey[:], op=ALU.add
+                                )
+
+                for m in range(ROW_TILES):
+                    numer_turned = turn_pool.tile([P, BLOCK], F32, tag="turn")
+                    for ct in range(COL_TILES):
+                        nc.tensor.transpose(
+                            numer_turned[:, ct * P : (ct + 1) * P], numer[:, ct, m * P : (m + 1) * P], ident[:]
+                        )
+                    out_sb = merge.tile([P, BLOCK], F32, tag="out_sb")
+                    nc.vector.tensor_tensor(out=out_sb[:], in0=numer_turned[:], in1=recip[:, m, :], op=ALU.mult)
+                    nc.sync.dma_start(
+                        out=out[m * P : (m + 1) * P, h * BLOCK : (h + 1) * BLOCK], in_=out_sb[:]
+                    )

@@ -272,6 +272,7 @@ def tile_vectormerge_pa_kernel(
                                     out=denom_turned[m][:, ct * P : (ct + 1) * P],
                                     lhsT=e[:, i, m * P : (m + 1) * P],
                                     rhs=ident[:],
+                                    is_transpose=True,
                                     start=(i == 0),
                                     stop=(i == GATES - 1),
                                 )
@@ -280,7 +281,7 @@ def tile_vectormerge_pa_kernel(
                     nc.scalar.activation(out=recip[:, m, :], in_=denom_turned[m][:], func=ACT.Ln)
                 nc.scalar.activation(out=recip[:], in_=recip[:], func=ACT.Exp, scale=-1.0)
 
-                numer = merge.tile([P, COL_TILES, ROWS], F32, tag="numer", bufs=1)
+                ey = [merge.tile([P, COL_TILES, ROWS], F32, tag="ey%d" % n, bufs=1, name="ey%d" % n) for n in range(3)]
                 for n in range(3):
                     own_passes = [qq for qq in all_passes if PASSES[qq][0] == n]
                     value_weights = {}
@@ -297,27 +298,23 @@ def tile_vectormerge_pa_kernel(
                             ct = 2 * pair + u
                             j = h * COL_TILES + ct
                             b_col = bias_cols[:, B_ROWS * n + j : B_ROWS * n + j + 1]
-                            if n == 0:
-                                nc.vector.scalar_tensor_tensor(
-                                    out=numer[:, ct, :], in0=y[:, u, :], scalar=b_col, in1=e_tiles[ct][:, n, :],
-                                    op0=ALU.add, op1=ALU.mult,
-                                )
-                            else:
-                                ey = merge.tile([P, ROWS], F32, tag="ey")
-                                nc.vector.scalar_tensor_tensor(
-                                    out=ey[:], in0=y[:, u, :], scalar=b_col, in1=e_tiles[ct][:, n, :],
-                                    op0=ALU.add, op1=ALU.mult,
-                                )
-                                nc.vector.tensor_tensor(
-                                    out=numer[:, ct, :], in0=numer[:, ct, :], in1=ey[:], op=ALU.add
-                                )
+                            nc.vector.scalar_tensor_tensor(
+                                out=ey[n][:, ct, :], in0=y[:, u, :], scalar=b_col, in1=e_tiles[ct][:, n, :],
+                                op0=ALU.add, op1=ALU.mult,
+                            )
 
                 for m in range(ROW_TILES):
                     numer_turned = turn_pool.tile([P, BLOCK], F32, tag="turn")
                     for ct in range(COL_TILES):
-                        nc.tensor.transpose(
-                            numer_turned[:, ct * P : (ct + 1) * P], numer[:, ct, m * P : (m + 1) * P], ident[:]
-                        )
+                        for n in range(3):
+                            nc.tensor.matmul(
+                                out=numer_turned[:, ct * P : (ct + 1) * P],
+                                lhsT=ey[n][:, ct, m * P : (m + 1) * P],
+                                rhs=ident[:],
+                                is_transpose=True,
+                                start=(n == 0),
+                                stop=(n == 2),
+                            )
                     out_sb = merge.tile([P, BLOCK], F32, tag="out_sb")
                     nc.vector.tensor_tensor(out=out_sb[:], in0=numer_turned[:], in1=recip[:, m, :], op=ALU.mult)
                     nc.sync.dma_start(

@@ -22,8 +22,9 @@ WIDTHS = (1024, 512, 2048)
 EPS = 1e-5
 BLOCK = 512
 BLOCKS = OUT // BLOCK
-COL_TILES = BLOCK // P
-PAIRS = COL_TILES // 2
+BLOCK_TILES = BLOCK // P
+COL_TILES = OUT // P
+PAIR = 2
 VECTOR_SHARE_16THS = 8
 BN_CHUNK = 512
 QUANTISE_WORDS = 1024
@@ -56,7 +57,7 @@ def tile_vectormerge_pa_kernel(
         const = stack.enter_context(tc.tile_pool(name="const", bufs=1))
         raw_pool = stack.enter_context(tc.tile_pool(name="raw", bufs=3))
         grouped_pool = stack.enter_context(tc.tile_pool(name="grouped", bufs=2))
-        codes_pool = stack.enter_context(tc.tile_pool(name="codes", bufs=len(PASSES)))
+        codes_pool = stack.enter_context(tc.tile_pool(name="codes", bufs=len(PASSES) + 2))
         acc_pool = stack.enter_context(tc.psum_pool(name="acc", bufs=6))
         turn_pool = stack.enter_context(tc.psum_pool(name="turn", bufs=2))
 
@@ -69,6 +70,8 @@ def tile_vectormerge_pa_kernel(
             x_sb.append(x_n)
         minus_half = const.tile([P, ROW_TILES], F32)
         nc.vector.memset(minus_half[:], -0.5)
+        table_loader = const.tile([P, 1], F32)
+        nc.scalar.activation(out=table_loader[:], in_=minus_half[:, 0:1], func=ACT.Exp)
         f_codes = const.tile([P, len(PASSES), ROWS], U32, align_bytes=64)
         f_scales = const.tile([P, len(PASSES), ROWS], U8, align_bytes=64)
 
@@ -182,22 +185,24 @@ def tile_vectormerge_pa_kernel(
                     )
                     q += 1
 
-        def quantise_weights(pieces, kind, bufs):
-            width = len(pieces) * BLOCK
-            raw = raw_pool.tile([P, PACK, width], BF16, tag="raw_" + kind)
-            for i, piece in enumerate(pieces):
+        def quantise_weights(pieces):
+            width = sum(piece.shape[1] for piece in pieces)
+            raw = raw_pool.tile([P, PACK, width], BF16, tag="raw")
+            col0 = 0
+            for piece in pieces:
+                cols = piece.shape[1]
                 nc.sync.dma_start(
-                    out=raw[:, :, i * BLOCK : (i + 1) * BLOCK],
-                    in_=piece.rearrange("(t p) w -> p t w", p=P),
+                    out=raw[:, :, col0 : col0 + cols], in_=piece.rearrange("(t p) w -> p t w", p=P)
                 )
-            grouped = grouped_pool.tile([P, width, PACK], BF16, tag="grouped_" + kind, align_bytes=64)
+                col0 += cols
+            grouped = grouped_pool.tile([P, width, PACK], BF16, tag="grouped", align_bytes=64)
             dst = grouped[:].rearrange("p (c i) t -> p c t i", i=4)
             src = raw[:].rearrange("p t (c i) -> p c t i", i=4)
             split = width * VECTOR_SHARE_16THS // 16 // 4
             nc.vector.tensor_copy(out=dst[:, 0:split], in_=src[:, 0:split])
             nc.scalar.copy(out=dst[:, split:], in_=src[:, split:])
-            codes = codes_pool.tile([P, width], U32, tag="codes_" + kind, align_bytes=64, bufs=bufs)
-            scales = codes_pool.tile([P, width], U8, tag="scales_" + kind, align_bytes=64, bufs=bufs)
+            codes = codes_pool.tile([P, width], U32, tag="codes", align_bytes=64)
+            scales = codes_pool.tile([P, width], U8, tag="scales", align_bytes=64)
             for col0 in range(0, width, QUANTISE_WORDS):
                 cols = min(QUANTISE_WORDS, width - col0)
                 nc.vector.quantize_mx(
@@ -220,30 +225,30 @@ def tile_vectormerge_pa_kernel(
                     stop=(i == len(passes) - 1),
                 )
 
+        def turn_sum(out, parts):
+            for i, part in enumerate(parts):
+                nc.tensor.matmul(
+                    out=out, lhsT=part, rhs=ident[:], is_transpose=True,
+                    start=(i == 0), stop=(i == len(parts) - 1),
+                )
+
         all_passes = list(range(len(PASSES)))
         with tc.tile_pool(name="merge", bufs=2) as merge:
+            e_tiles = []
             for h in range(BLOCKS):
                 gate_weights = []
                 for n, c in PASSES:
                     k_rows = slice(c * K_PASS, (c + 1) * K_PASS)
                     gate_weights.append(quantise_weights(
-                        [Wgs[n][k_rows, i * OUT + h * BLOCK : i * OUT + (h + 1) * BLOCK] for i in range(GATES)],
-                        "gates", len(PASSES) + 2,
+                        [Wgs[n][k_rows, i * OUT + h * BLOCK : i * OUT + (h + 1) * BLOCK] for i in range(GATES)]
                     ))
-
-                denom_turned = [
-                    turn_pool.tile([P, BLOCK], F32, tag="turn", name="denom_turned%d" % m)
-                    for m in range(ROW_TILES)
-                ]
-                e_tiles = []
-                for pair in range(PAIRS):
-                    logits = [acc_pool.tile([P, 2, ROWS], F32, tag="acc", name="logits%d" % i) for i in range(GATES)]
-                    for u in range(2):
+                for pair in range(BLOCK_TILES // PAIR):
+                    logits = [acc_pool.tile([P, PAIR, ROWS], F32, tag="acc", name="logits%d" % i) for i in range(GATES)]
+                    for u in range(PAIR):
                         for i in range(GATES):
-                            product(logits[i][:, u, :], gate_weights, i * BLOCK + (2 * pair + u) * P, all_passes)
-                    for u in range(2):
-                        ct = 2 * pair + u
-                        j = h * COL_TILES + ct
+                            product(logits[i][:, u, :], gate_weights, i * BLOCK + (PAIR * pair + u) * P, all_passes)
+                    for u in range(PAIR):
+                        j = h * BLOCK_TILES + PAIR * pair + u
                         bg = [bg_sum[:, B_ROWS * i + j : B_ROWS * i + j + 1] for i in range(GATES)]
                         l0 = merge.tile([P, ROWS], F32, tag="l0")
                         nc.scalar.activation(out=l0[:], in_=logits[0][:, u, :], func=ACT.Identity, bias=bg[0])
@@ -266,57 +271,55 @@ def tile_vectormerge_pa_kernel(
                             )
                         nc.scalar.activation(out=e[:], in_=e[:], func=ACT.Exp)
                         e_tiles.append(e)
-                        for m in range(ROW_TILES):
-                            for i in range(GATES):
-                                nc.tensor.matmul(
-                                    out=denom_turned[m][:, ct * P : (ct + 1) * P],
-                                    lhsT=e[:, i, m * P : (m + 1) * P],
-                                    rhs=ident[:],
-                                    is_transpose=True,
-                                    start=(i == 0),
-                                    stop=(i == GATES - 1),
-                                )
-                recip = merge.tile([P, ROW_TILES, BLOCK], F32, tag="recip", bufs=1)
-                for m in range(ROW_TILES):
-                    nc.scalar.activation(out=recip[:, m, :], in_=denom_turned[m][:], func=ACT.Ln)
-                nc.scalar.activation(out=recip[:], in_=recip[:], func=ACT.Exp, scale=-1.0)
 
-                ey = [merge.tile([P, COL_TILES, ROWS], F32, tag="ey%d" % n, bufs=1, name="ey%d" % n) for n in range(3)]
-                for n in range(3):
-                    own_passes = [qq for qq in all_passes if PASSES[qq][0] == n]
-                    value_weights = {}
-                    for qq in own_passes:
-                        c = PASSES[qq][1]
-                        value_weights[qq] = quantise_weights(
-                            [Ws[n][c * K_PASS : (c + 1) * K_PASS, h * BLOCK : (h + 1) * BLOCK]], "values", len(PASSES)
+            recip = merge.tile([P, COL_TILES // PAIR, ROW_TILES, PAIR, P], F32, tag="recip", bufs=1)
+            zero = merge.tile([P, 1], F32, tag="zero", bufs=1)
+            nc.vector.tensor_scalar(
+                out=zero[:], in0=e_tiles[-1][:, 0, 0:1], scalar1=0.0, scalar2=None, op0=ALU.mult
+            )
+            for pair in range(COL_TILES // PAIR):
+                denom = turn_pool.tile([P, ROW_TILES, PAIR, P], F32, tag="turn")
+                for m in range(ROW_TILES):
+                    for u in range(PAIR):
+                        e = e_tiles[PAIR * pair + u]
+                        turn_sum(denom[:, m, u, :], [e[:, i, m * P : (m + 1) * P] for i in range(GATES)])
+                nc.scalar.activation(out=recip[:, pair], in_=denom[:], func=ACT.Ln, bias=zero[:])
+            for pair in range(COL_TILES // PAIR):
+                nc.scalar.activation(out=recip[:, pair], in_=recip[:, pair], func=ACT.Exp, scale=-1.0)
+
+            weighted = [
+                merge.tile([P, COL_TILES, ROWS], F32, tag="weighted%d" % n, bufs=1, name="weighted%d" % n)
+                for n in range(3)
+            ]
+            for n in (2, 0, 1):
+                own_passes = [q for q in all_passes if PASSES[q][0] == n]
+                value_weights = {}
+                for q in own_passes:
+                    c = PASSES[q][1]
+                    value_weights[q] = quantise_weights([Ws[n][c * K_PASS : (c + 1) * K_PASS, :]])
+                for pair in range(COL_TILES // PAIR):
+                    y = acc_pool.tile([P, PAIR, ROWS], F32, tag="acc")
+                    for u in range(PAIR):
+                        product(y[:, u, :], value_weights, (PAIR * pair + u) * P, own_passes)
+                    for u in range(PAIR):
+                        j = PAIR * pair + u
+                        nc.vector.scalar_tensor_tensor(
+                            out=weighted[n][:, j, :], in0=y[:, u, :],
+                            scalar=bias_cols[:, B_ROWS * n + j : B_ROWS * n + j + 1],
+                            in1=e_tiles[j][:, n, :], op0=ALU.add, op1=ALU.mult,
                         )
-                    for pair in range(PAIRS):
-                        y = acc_pool.tile([P, 2, ROWS], F32, tag="acc")
-                        for u in range(2):
-                            product(y[:, u, :], value_weights, (2 * pair + u) * P, own_passes)
-                        for u in range(2):
-                            ct = 2 * pair + u
-                            j = h * COL_TILES + ct
-                            b_col = bias_cols[:, B_ROWS * n + j : B_ROWS * n + j + 1]
-                            nc.vector.scalar_tensor_tensor(
-                                out=ey[n][:, ct, :], in0=y[:, u, :], scalar=b_col, in1=e_tiles[ct][:, n, :],
-                                op0=ALU.add, op1=ALU.mult,
-                            )
 
+            for pair in range(COL_TILES // PAIR):
+                numer = turn_pool.tile([P, ROW_TILES, PAIR, P], F32, tag="turn")
                 for m in range(ROW_TILES):
-                    numer_turned = turn_pool.tile([P, BLOCK], F32, tag="turn")
-                    for ct in range(COL_TILES):
-                        for n in range(3):
-                            nc.tensor.matmul(
-                                out=numer_turned[:, ct * P : (ct + 1) * P],
-                                lhsT=ey[n][:, ct, m * P : (m + 1) * P],
-                                rhs=ident[:],
-                                is_transpose=True,
-                                start=(n == 0),
-                                stop=(n == 2),
-                            )
-                    out_sb = merge.tile([P, BLOCK], F32, tag="out_sb")
-                    nc.vector.tensor_tensor(out=out_sb[:], in0=numer_turned[:], in1=recip[:, m, :], op=ALU.mult)
-                    nc.sync.dma_start(
-                        out=out[m * P : (m + 1) * P, h * BLOCK : (h + 1) * BLOCK], in_=out_sb[:]
-                    )
+                    for u in range(PAIR):
+                        j = PAIR * pair + u
+                        turn_sum(
+                            numer[:, m, u, :], [weighted[n][:, j, m * P : (m + 1) * P] for n in range(3)]
+                        )
+                out_sb = merge.tile([P, ROW_TILES, PAIR, P], F32, tag="out_sb", bufs=COL_TILES // PAIR)
+                nc.vector.tensor_tensor(out=out_sb[:], in0=numer[:], in1=recip[:, pair], op=ALU.mult)
+                nc.sync.dma_start(
+                    out=out[:, pair * PAIR * P : (pair + 1) * PAIR * P].rearrange("(m p) c -> p m c", p=P),
+                    in_=out_sb[:].rearrange("p m u c -> p m (u c)"),
+                )

@@ -29,7 +29,8 @@ VECTOR_SHARE_16THS = 8
 BN_CHUNK = 512
 QUANTISE_WORDS = 1024
 
-PASSES = tuple((n, c) for n in range(3) for c in range(WIDTHS[n] // K_PASS))
+STREAM_ORDER = (1, 0, 2)
+PASSES = tuple((n, c) for n in STREAM_ORDER for c in range(WIDTHS[n] // K_PASS))
 K_TILES = sum(WIDTHS) // P
 
 FLOPS = 2 * ROWS * sum(WIDTHS) * (OUT + GATES * OUT)
@@ -63,11 +64,32 @@ def tile_vectormerge_pa_kernel(
 
         ident = const.tile([P, P], F32)
         make_identity(nc, ident[:])
-        x_sb = []
-        for n in range(3):
-            x_n = const.tile([P, ROW_TILES, WIDTHS[n]], BF16, name="x%d" % n)
-            nc.gpsimd.dma_start(out=x_n[:], in_=xs[n].rearrange("(m p) d -> p m d", p=P))
-            x_sb.append(x_n)
+        x_sb = [const.tile([P, ROW_TILES, WIDTHS[n]], BF16, name="x%d" % n) for n in range(3)]
+
+        def load_weights(pieces):
+            width = sum(piece.shape[1] for piece in pieces)
+            raw = raw_pool.tile([P, PACK, width], BF16, tag="raw")
+            col0 = 0
+            for piece in pieces:
+                cols = piece.shape[1]
+                nc.sync.dma_start(
+                    out=raw[:, :, col0 : col0 + cols], in_=piece.rearrange("(t p) w -> p t w", p=P)
+                )
+                col0 += cols
+            return raw
+
+        def load_gates(h, q):
+            n, c = PASSES[q]
+            k_rows = slice(c * K_PASS, (c + 1) * K_PASS)
+            return load_weights(
+                [Wgs[n][k_rows, i * OUT + h * BLOCK : i * OUT + (h + 1) * BLOCK] for i in range(GATES)]
+            )
+
+        loaded = {}
+        for n in STREAM_ORDER:
+            if n == STREAM_ORDER[-1]:
+                loaded[0, 0] = load_gates(0, 0)
+            nc.sync.dma_start(out=x_sb[n][:], in_=xs[n].rearrange("(m p) d -> p m d", p=P))
         minus_half = const.tile([P, ROW_TILES], F32)
         nc.vector.memset(minus_half[:], -0.5)
         table_loader = const.tile([P, 1], F32)
@@ -80,23 +102,23 @@ def tile_vectormerge_pa_kernel(
         nc.vector.memset(ln_rows[:], 0.0)
         nc.vector.memset(bias_rows[:], 0.0)
         k_tile0 = 0
-        for n in range(3):
+        for n in STREAM_ORDER:
             k_tiles = WIDTHS[n] // P
-            nc.sync.dma_start(
+            nc.scalar.dma_start(
                 out=ln_rows[k_tile0 : k_tile0 + k_tiles, :],
                 in_=ln_ws[n].rearrange("(r c) -> r c", c=P),
             )
-            nc.sync.dma_start(
+            nc.scalar.dma_start(
                 out=ln_rows[K_TILES + k_tile0 : K_TILES + k_tile0 + k_tiles, :],
                 in_=ln_bs[n].rearrange("(r c) -> r c", c=P),
             )
             k_tile0 += k_tiles
         for n in range(3):
-            nc.gpsimd.dma_start(
+            nc.scalar.dma_start(
                 out=bias_rows[n * B_ROWS : (n + 1) * B_ROWS, :],
                 in_=bs[n].rearrange("(r c) -> r c", c=P),
             )
-            nc.gpsimd.dma_start(
+            nc.scalar.dma_start(
                 out=bias_rows[3 * B_ROWS + n * BG_ROWS : 3 * B_ROWS + (n + 1) * BG_ROWS, :],
                 in_=bgs[n].rearrange("(r c) -> r c", c=P),
             )
@@ -111,25 +133,14 @@ def tile_vectormerge_pa_kernel(
             return columns
 
         ln_cols = to_columns(ln_rows, "ln")
-        bias_cols = to_columns(bias_rows, "bias")
-        bg_sum = const.tile([P, BG_ROWS], F32)
-        bg0 = 3 * B_ROWS
-        nc.vector.tensor_tensor(
-            out=bg_sum[:], in0=bias_cols[:, bg0 : bg0 + BG_ROWS],
-            in1=bias_cols[:, bg0 + BG_ROWS : bg0 + 2 * BG_ROWS], op=ALU.add,
-        )
-        nc.vector.tensor_tensor(
-            out=bg_sum[:], in0=bg_sum[:],
-            in1=bias_cols[:, bg0 + 2 * BG_ROWS : bg0 + 3 * BG_ROWS], op=ALU.add,
-        )
 
         with tc.tile_pool(name="norm", bufs=2) as norm:
             q = 0
-            for n in range(3):
+            for n in STREAM_ORDER:
                 d = WIDTHS[n]
                 chunks = d // BN_CHUNK
                 stats = norm.tile([P, ROW_TILES, chunks, 6], F32, name="stats%d" % n, bufs=1)
-                mean_var = norm.tile([P, ROW_TILES, 2], F32, tag="mean_var")
+                mean_var = norm.tile([P, ROW_TILES, 2], F32, tag="mean_var", bufs=3)
                 for m in range(ROW_TILES):
                     for j in range(chunks):
                         nc.vector.bn_stats(
@@ -139,15 +150,14 @@ def tile_vectormerge_pa_kernel(
                     nc.vector.bn_aggr(
                         out=mean_var[:, m, :], in_=stats[:, m, :, :].rearrange("p c s -> p (c s)")
                     )
-                var_eps = norm.tile([P, ROW_TILES], F32, tag="var_eps")
+                var_eps = norm.tile([P, ROW_TILES], F32, tag="var_eps", bufs=3)
                 nc.vector.tensor_scalar_add(out=var_eps[:], in0=mean_var[:, :, 1], scalar1=EPS)
-                rstd = norm.tile([P, ROW_TILES], F32, tag="rstd")
+                minus_mean = norm.tile([P, ROW_TILES], F32, tag="minus_mean", bufs=3)
+                nc.vector.tensor_scalar_mul(out=minus_mean[:], in0=mean_var[:, :, 0], scalar1=-1.0)
+                rstd = norm.tile([P, ROW_TILES], F32, tag="rstd", bufs=3)
                 nc.gpsimd.tensor_tensor(out=rstd[:], in0=var_eps[:], in1=minus_half[:], op=ALU.pow)
-                shift = norm.tile([P, ROW_TILES], F32, tag="shift")
-                nc.vector.scalar_tensor_tensor(
-                    out=shift[:], in0=mean_var[:, :, 0], scalar=-1.0, in1=rstd[:],
-                    op0=ALU.mult, op1=ALU.mult,
-                )
+                shift = norm.tile([P, ROW_TILES], F32, tag="shift", bufs=3)
+                nc.gpsimd.tensor_tensor(out=shift[:], in0=minus_mean[:], in1=rstd[:], op=ALU.mult)
                 for c in range(d // K_PASS):
                     z = []
                     for m in range(ROW_TILES):
@@ -185,16 +195,20 @@ def tile_vectormerge_pa_kernel(
                     )
                     q += 1
 
-        def quantise_weights(pieces):
-            width = sum(piece.shape[1] for piece in pieces)
-            raw = raw_pool.tile([P, PACK, width], BF16, tag="raw")
-            col0 = 0
-            for piece in pieces:
-                cols = piece.shape[1]
-                nc.sync.dma_start(
-                    out=raw[:, :, col0 : col0 + cols], in_=piece.rearrange("(t p) w -> p t w", p=P)
-                )
-                col0 += cols
+        bias_cols = to_columns(bias_rows, "bias")
+        bg_sum = const.tile([P, BG_ROWS], F32)
+        bg0 = 3 * B_ROWS
+        nc.vector.tensor_tensor(
+            out=bg_sum[:], in0=bias_cols[:, bg0 : bg0 + BG_ROWS],
+            in1=bias_cols[:, bg0 + BG_ROWS : bg0 + 2 * BG_ROWS], op=ALU.add,
+        )
+        nc.vector.tensor_tensor(
+            out=bg_sum[:], in0=bg_sum[:],
+            in1=bias_cols[:, bg0 + 2 * BG_ROWS : bg0 + 3 * BG_ROWS], op=ALU.add,
+        )
+
+        def quantise_weights(raw):
+            width = raw.shape[2]
             grouped = grouped_pool.tile([P, width, PACK], BF16, tag="grouped", align_bytes=64)
             dst = grouped[:].rearrange("p (c i) t -> p c t i", i=4)
             src = raw[:].rearrange("p t (c i) -> p c t i", i=4)
@@ -237,11 +251,9 @@ def tile_vectormerge_pa_kernel(
             e_tiles = []
             for h in range(BLOCKS):
                 gate_weights = []
-                for n, c in PASSES:
-                    k_rows = slice(c * K_PASS, (c + 1) * K_PASS)
-                    gate_weights.append(quantise_weights(
-                        [Wgs[n][k_rows, i * OUT + h * BLOCK : i * OUT + (h + 1) * BLOCK] for i in range(GATES)]
-                    ))
+                for q in all_passes:
+                    raw = loaded[h, q] if (h, q) in loaded else load_gates(h, q)
+                    gate_weights.append(quantise_weights(raw))
                 for pair in range(BLOCK_TILES // PAIR):
                     logits = [acc_pool.tile([P, PAIR, ROWS], F32, tag="acc", name="logits%d" % i) for i in range(GATES)]
                     for u in range(PAIR):
@@ -296,7 +308,7 @@ def tile_vectormerge_pa_kernel(
                 value_weights = {}
                 for q in own_passes:
                     c = PASSES[q][1]
-                    value_weights[q] = quantise_weights([Ws[n][c * K_PASS : (c + 1) * K_PASS, :]])
+                    value_weights[q] = quantise_weights(load_weights([Ws[n][c * K_PASS : (c + 1) * K_PASS, :]]))
                 for pair in range(COL_TILES // PAIR):
                     y = acc_pool.tile([P, PAIR, ROWS], F32, tag="acc")
                     for u in range(PAIR):

@@ -25,7 +25,8 @@ BLOCKS = OUT // BLOCK
 BLOCK_TILES = BLOCK // P
 COL_TILES = OUT // P
 PAIR = 2
-VECTOR_SHARE_16THS = 8
+VECTOR_SHARE_GATES = 8
+VECTOR_SHARE_VALUES = 11
 BN_CHUNK = 512
 QUANTISE_WORDS = 1024
 
@@ -64,6 +65,8 @@ def tile_vectormerge_pa_kernel(
 
         ident = const.tile([P, P], F32)
         make_identity(nc, ident[:])
+        minus_ident = const.tile([P, P], F32)
+        nc.vector.tensor_scalar_mul(out=minus_ident[:], in0=ident[:], scalar1=-1.0)
         x_sb = [const.tile([P, ROW_TILES, WIDTHS[n]], BF16, name="x%d" % n) for n in range(3)]
 
         def load_weights(pieces):
@@ -207,12 +210,12 @@ def tile_vectormerge_pa_kernel(
             in1=bias_cols[:, bg0 + 2 * BG_ROWS : bg0 + 3 * BG_ROWS], op=ALU.add,
         )
 
-        def quantise_weights(raw):
+        def quantise_weights(raw, vector_share):
             width = raw.shape[2]
             grouped = grouped_pool.tile([P, width, PACK], BF16, tag="grouped", align_bytes=64)
             dst = grouped[:].rearrange("p (c i) t -> p c t i", i=4)
             src = raw[:].rearrange("p t (c i) -> p c t i", i=4)
-            split = width * VECTOR_SHARE_16THS // 16 // 4
+            split = width * vector_share // 16 // 4
             nc.vector.tensor_copy(out=dst[:, 0:split], in_=src[:, 0:split])
             nc.scalar.copy(out=dst[:, split:], in_=src[:, split:])
             codes = codes_pool.tile([P, width], U32, tag="codes", align_bytes=64)
@@ -226,18 +229,17 @@ def tile_vectormerge_pa_kernel(
                 )
             return codes, scales
 
-        def product(acc, weights, col0, passes):
-            for i, qq in enumerate(passes):
-                codes, scales = weights[qq]
-                nc.tensor.matmul_mx(
-                    out=acc,
-                    lhsT=codes[:, col0 : col0 + P].bitcast(FP8X4),
-                    lhsT_scale=scales[:, col0 : col0 + P],
-                    rhs=f_codes[:, qq, :].bitcast(FP8X4),
-                    rhs_scale=f_scales[:, qq, :],
-                    start=(i == 0),
-                    stop=(i == len(passes) - 1),
-                )
+        def add_pass(acc, weights, col0, q, passes):
+            codes, scales = weights
+            nc.tensor.matmul_mx(
+                out=acc,
+                lhsT=codes[:, col0 : col0 + P].bitcast(FP8X4),
+                lhsT_scale=scales[:, col0 : col0 + P],
+                rhs=f_codes[:, q, :].bitcast(FP8X4),
+                rhs_scale=f_scales[:, q, :],
+                start=(q == passes[0]),
+                stop=(q == passes[-1]),
+            )
 
         def turn_sum(out, parts):
             for i, part in enumerate(parts):
@@ -248,56 +250,65 @@ def tile_vectormerge_pa_kernel(
 
         all_passes = list(range(len(PASSES)))
         with tc.tile_pool(name="merge", bufs=2) as merge:
-            e_tiles = []
+            e_pairs = []
             for h in range(BLOCKS):
+                block_logits = [
+                    [acc_pool.tile([P, PAIR, ROWS], F32, tag="acc", name="logits%d" % i) for i in range(GATES)]
+                    for pair in range(BLOCK_TILES // PAIR)
+                ]
                 gate_weights = []
                 for q in all_passes:
                     raw = loaded[h, q] if (h, q) in loaded else load_gates(h, q)
-                    gate_weights.append(quantise_weights(raw))
-                for pair in range(BLOCK_TILES // PAIR):
-                    logits = [acc_pool.tile([P, PAIR, ROWS], F32, tag="acc", name="logits%d" % i) for i in range(GATES)]
-                    for u in range(PAIR):
+                    gate_weights.append(quantise_weights(raw, VECTOR_SHARE_GATES))
+                    for pair, logits in enumerate(block_logits):
                         for i in range(GATES):
-                            product(logits[i][:, u, :], gate_weights, i * BLOCK + (PAIR * pair + u) * P, all_passes)
+                            add_pass(logits[i][:, 0, :], gate_weights[q], i * BLOCK + PAIR * pair * P, q, all_passes)
+                for pair, logits in enumerate(block_logits):
+                    for i in range(GATES):
+                        for q in all_passes:
+                            col0 = i * BLOCK + (PAIR * pair + 1) * P
+                            add_pass(logits[i][:, 1, :], gate_weights[q], col0, q, all_passes)
+                    diff = merge.tile([P, GATES - 1, PAIR, ROWS], F32, tag="diff")
                     for u in range(PAIR):
                         j = h * BLOCK_TILES + PAIR * pair + u
                         bg = [bg_sum[:, B_ROWS * i + j : B_ROWS * i + j + 1] for i in range(GATES)]
                         l0 = merge.tile([P, ROWS], F32, tag="l0")
                         nc.scalar.activation(out=l0[:], in_=logits[0][:, u, :], func=ACT.Identity, bias=bg[0])
-                        top01 = merge.tile([P, ROWS], F32, tag="top01")
-                        nc.vector.scalar_tensor_tensor(
-                            out=top01[:], in0=logits[1][:, u, :], scalar=bg[1], in1=l0[:],
-                            op0=ALU.add, op1=ALU.max,
-                        )
-                        top = merge.tile([P, ROWS], F32, tag="top")
-                        nc.vector.scalar_tensor_tensor(
-                            out=top[:], in0=logits[2][:, u, :], scalar=bg[2], in1=top01[:],
-                            op0=ALU.add, op1=ALU.max,
-                        )
-                        e = merge.tile([P, GATES, ROWS], F32, tag="e", bufs=COL_TILES)
-                        nc.vector.tensor_tensor(out=e[:, 0, :], in0=l0[:], in1=top[:], op=ALU.subtract)
                         for i in (1, 2):
                             nc.vector.scalar_tensor_tensor(
-                                out=e[:, i, :], in0=logits[i][:, u, :], scalar=bg[i], in1=top[:],
+                                out=diff[:, i - 1, u, :], in0=logits[i][:, u, :], scalar=bg[i], in1=l0[:],
                                 op0=ALU.add, op1=ALU.subtract,
                             )
-                        nc.scalar.activation(out=e[:], in_=e[:], func=ACT.Exp)
-                        e_tiles.append(e)
+                    top = merge.tile([P, PAIR, ROWS], F32, tag="top")
+                    nc.vector.scalar_tensor_tensor(
+                        out=top[:], in0=diff[:, 0], scalar=0.0, in1=diff[:, 1], op0=ALU.max, op1=ALU.max
+                    )
+                    e = merge.tile([P, GATES, PAIR, ROWS], F32, tag="e", bufs=COL_TILES // PAIR)
+                    nc.scalar.activation(out=e[:, 0], in_=top[:], func=ACT.Exp, scale=-1.0)
+                    for i in (1, 2):
+                        for u in range(PAIR):
+                            nc.tensor.matmul(
+                                out=logits[i][:, u, :], lhsT=ident[:], rhs=diff[:, i - 1, u, :], start=True, stop=False
+                            )
+                            nc.tensor.matmul(
+                                out=logits[i][:, u, :], lhsT=minus_ident[:], rhs=top[:, u, :], start=False, stop=True
+                            )
+                        nc.scalar.activation(out=e[:, i], in_=logits[i][:], func=ACT.Exp)
+                    e_pairs.append(e)
 
             recip = merge.tile([P, COL_TILES // PAIR, ROW_TILES, PAIR, P], F32, tag="recip", bufs=1)
             zero = merge.tile([P, 1], F32, tag="zero", bufs=1)
             nc.vector.tensor_scalar(
-                out=zero[:], in0=e_tiles[-1][:, 0, 0:1], scalar1=0.0, scalar2=None, op0=ALU.mult
+                out=zero[:], in0=e_pairs[-1][:, GATES - 1, 0, 0:1], scalar1=0.0, scalar2=None, op0=ALU.mult
             )
             for pair in range(COL_TILES // PAIR):
                 denom = turn_pool.tile([P, ROW_TILES, PAIR, P], F32, tag="turn")
                 for m in range(ROW_TILES):
                     for u in range(PAIR):
-                        e = e_tiles[PAIR * pair + u]
-                        turn_sum(denom[:, m, u, :], [e[:, i, m * P : (m + 1) * P] for i in range(GATES)])
+                        e = e_pairs[pair]
+                        turn_sum(denom[:, m, u, :], [e[:, i, u, m * P : (m + 1) * P] for i in range(GATES)])
                 nc.scalar.activation(out=recip[:, pair], in_=denom[:], func=ACT.Ln, bias=zero[:])
-            for pair in range(COL_TILES // PAIR):
-                nc.scalar.activation(out=recip[:, pair], in_=recip[:, pair], func=ACT.Exp, scale=-1.0)
+            nc.scalar.activation(out=recip[:], in_=recip[:], func=ACT.Exp, scale=-1.0)
 
             weighted = [
                 merge.tile([P, COL_TILES, ROWS], F32, tag="weighted%d" % n, bufs=1, name="weighted%d" % n)
@@ -308,21 +319,23 @@ def tile_vectormerge_pa_kernel(
                 value_weights = {}
                 for q in own_passes:
                     c = PASSES[q][1]
-                    value_weights[q] = quantise_weights(load_weights([Ws[n][c * K_PASS : (c + 1) * K_PASS, :]]))
+                    raw = load_weights([Ws[n][c * K_PASS : (c + 1) * K_PASS, :]])
+                    value_weights[q] = quantise_weights(raw, VECTOR_SHARE_VALUES)
                 for pair in range(COL_TILES // PAIR):
                     y = acc_pool.tile([P, PAIR, ROWS], F32, tag="acc")
                     for u in range(PAIR):
-                        product(y[:, u, :], value_weights, (PAIR * pair + u) * P, own_passes)
+                        for q in own_passes:
+                            add_pass(y[:, u, :], value_weights[q], (PAIR * pair + u) * P, q, own_passes)
                     for u in range(PAIR):
                         j = PAIR * pair + u
                         nc.vector.scalar_tensor_tensor(
                             out=weighted[n][:, j, :], in0=y[:, u, :],
                             scalar=bias_cols[:, B_ROWS * n + j : B_ROWS * n + j + 1],
-                            in1=e_tiles[j][:, n, :], op0=ALU.add, op1=ALU.mult,
+                            in1=e_pairs[pair][:, n, u, :], op0=ALU.add, op1=ALU.mult,
                         )
 
             for pair in range(COL_TILES // PAIR):
-                numer = turn_pool.tile([P, ROW_TILES, PAIR, P], F32, tag="turn")
+                numer = acc_pool.tile([P, ROW_TILES, PAIR, P], F32, tag="acc")
                 for m in range(ROW_TILES):
                     for u in range(PAIR):
                         j = PAIR * pair + u

@@ -57,8 +57,8 @@ def tile_vectormerge_pa_kernel(
 
     with ExitStack() as stack:
         const = stack.enter_context(tc.tile_pool(name="const", bufs=1))
-        raw_pool = stack.enter_context(tc.tile_pool(name="raw", bufs=3))
-        grouped_pool = stack.enter_context(tc.tile_pool(name="grouped", bufs=2))
+        raw_pool = stack.enter_context(tc.tile_pool(name="raw", bufs=4))
+        grouped_pool = stack.enter_context(tc.tile_pool(name="grouped", bufs=3))
         codes_pool = stack.enter_context(tc.tile_pool(name="codes", bufs=len(PASSES) + 2))
         acc_pool = stack.enter_context(tc.psum_pool(name="acc", bufs=6))
         turn_pool = stack.enter_context(tc.psum_pool(name="turn", bufs=2))
@@ -310,10 +310,6 @@ def tile_vectormerge_pa_kernel(
                 nc.scalar.activation(out=recip[:, pair], in_=denom[:], func=ACT.Ln, bias=zero[:])
             nc.scalar.activation(out=recip[:], in_=recip[:], func=ACT.Exp, scale=-1.0)
 
-            weighted = [
-                merge.tile([P, COL_TILES, ROWS], F32, tag="weighted%d" % n, bufs=1, name="weighted%d" % n)
-                for n in range(3)
-            ]
             for n in (2, 0, 1):
                 own_passes = [q for q in all_passes if PASSES[q][0] == n]
                 value_weights = {}
@@ -328,20 +324,18 @@ def tile_vectormerge_pa_kernel(
                             add_pass(y[:, u, :], value_weights[q], (PAIR * pair + u) * P, q, own_passes)
                     for u in range(PAIR):
                         j = PAIR * pair + u
+                        e_n = e_pairs[pair][:, n, u, :]
                         nc.vector.scalar_tensor_tensor(
-                            out=weighted[n][:, j, :], in0=y[:, u, :],
-                            scalar=bias_cols[:, B_ROWS * n + j : B_ROWS * n + j + 1],
-                            in1=e_pairs[pair][:, n, u, :], op0=ALU.add, op1=ALU.mult,
+                            out=e_n, in0=y[:, u, :], scalar=bias_cols[:, B_ROWS * n + j : B_ROWS * n + j + 1],
+                            in1=e_n, op0=ALU.add, op1=ALU.mult,
                         )
 
             for pair in range(COL_TILES // PAIR):
                 numer = acc_pool.tile([P, ROW_TILES, PAIR, P], F32, tag="acc")
                 for m in range(ROW_TILES):
                     for u in range(PAIR):
-                        j = PAIR * pair + u
-                        turn_sum(
-                            numer[:, m, u, :], [weighted[n][:, j, m * P : (m + 1) * P] for n in range(3)]
-                        )
+                        e = e_pairs[pair]
+                        turn_sum(numer[:, m, u, :], [e[:, n, u, m * P : (m + 1) * P] for n in range(3)])
                 out_sb = merge.tile([P, ROW_TILES, PAIR, P], F32, tag="out_sb", bufs=COL_TILES // PAIR)
                 nc.vector.tensor_tensor(out=out_sb[:], in0=numer[:], in1=recip[:, pair], op=ALU.mult)
                 nc.sync.dma_start(

@@ -93,10 +93,10 @@ def tile_vectormerge_pa_kernel(
             if n == STREAM_ORDER[-1]:
                 loaded[0, 0] = load_gates(0, 0)
             nc.sync.dma_start(out=x_sb[n][:], in_=xs[n].rearrange("(m p) d -> p m d", p=P))
-        minus_half = const.tile([P, ROW_TILES], F32)
-        nc.vector.memset(minus_half[:], -0.5)
+        one = const.tile([P, 1], F32)
+        nc.vector.memset(one[:], 1.0)
         table_loader = const.tile([P, 1], F32)
-        nc.scalar.activation(out=table_loader[:], in_=minus_half[:, 0:1], func=ACT.Exp)
+        nc.scalar.activation(out=table_loader[:], in_=one[:], func=ACT.Sqrt)
         f_codes = const.tile([P, len(PASSES), ROWS], U32, align_bytes=64)
         f_scales = const.tile([P, len(PASSES), ROWS], U8, align_bytes=64)
 
@@ -116,16 +116,6 @@ def tile_vectormerge_pa_kernel(
                 in_=ln_bs[n].rearrange("(r c) -> r c", c=P),
             )
             k_tile0 += k_tiles
-        for n in range(3):
-            nc.scalar.dma_start(
-                out=bias_rows[n * B_ROWS : (n + 1) * B_ROWS, :],
-                in_=bs[n].rearrange("(r c) -> r c", c=P),
-            )
-            nc.scalar.dma_start(
-                out=bias_rows[3 * B_ROWS + n * BG_ROWS : 3 * B_ROWS + (n + 1) * BG_ROWS, :],
-                in_=bgs[n].rearrange("(r c) -> r c", c=P),
-            )
-
         def to_columns(rows_bf16, name):
             rows_f32 = const.tile([P, P], F32, name=name + "_f32")
             nc.vector.tensor_copy(out=rows_f32[:], in_=rows_bf16[:])
@@ -157,10 +147,12 @@ def tile_vectormerge_pa_kernel(
                 nc.vector.tensor_scalar_add(out=var_eps[:], in0=mean_var[:, :, 1], scalar1=EPS)
                 minus_mean = norm.tile([P, ROW_TILES], F32, tag="minus_mean", bufs=3)
                 nc.vector.tensor_scalar_mul(out=minus_mean[:], in0=mean_var[:, :, 0], scalar1=-1.0)
+                sigma = norm.tile([P, ROW_TILES], F32, tag="sigma", bufs=3)
+                nc.scalar.activation(out=sigma[:], in_=var_eps[:], func=ACT.Sqrt)
                 rstd = norm.tile([P, ROW_TILES], F32, tag="rstd", bufs=3)
-                nc.gpsimd.tensor_tensor(out=rstd[:], in0=var_eps[:], in1=minus_half[:], op=ALU.pow)
+                nc.vector.reciprocal(out=rstd[:], in_=sigma[:])
                 shift = norm.tile([P, ROW_TILES], F32, tag="shift", bufs=3)
-                nc.gpsimd.tensor_tensor(out=shift[:], in0=minus_mean[:], in1=rstd[:], op=ALU.mult)
+                nc.vector.tensor_tensor(out=shift[:], in0=minus_mean[:], in1=rstd[:], op=ALU.mult)
                 for c in range(d // K_PASS):
                     z = []
                     for m in range(ROW_TILES):
@@ -197,6 +189,16 @@ def tile_vectormerge_pa_kernel(
                         in_=f_grouped[:].rearrange("p r t -> p (r t)"),
                     )
                     q += 1
+
+        for n in range(3):
+            nc.sync.dma_start(
+                out=bias_rows[n * B_ROWS : (n + 1) * B_ROWS, :],
+                in_=bs[n].rearrange("(r c) -> r c", c=P),
+            )
+            nc.sync.dma_start(
+                out=bias_rows[3 * B_ROWS + n * BG_ROWS : 3 * B_ROWS + (n + 1) * BG_ROWS, :],
+                in_=bgs[n].rearrange("(r c) -> r c", c=P),
+            )
 
         bias_cols = to_columns(bias_rows, "bias")
         bg_sum = const.tile([P, BG_ROWS], F32)

@@ -25,8 +25,8 @@ BLOCKS = OUT // BLOCK
 BLOCK_TILES = BLOCK // P
 COL_TILES = OUT // P
 PAIR = 2
-VECTOR_SHARE_GATES = 8
-VECTOR_SHARE_VALUES = 11
+VECTOR_SHARE_GATES = (8, 9)
+VECTOR_SHARE_VALUES = 9
 BN_CHUNK = 512
 QUANTISE_WORDS = 1024
 
@@ -261,7 +261,7 @@ def tile_vectormerge_pa_kernel(
                 gate_weights = []
                 for q in all_passes:
                     raw = loaded[h, q] if (h, q) in loaded else load_gates(h, q)
-                    gate_weights.append(quantise_weights(raw, VECTOR_SHARE_GATES))
+                    gate_weights.append(quantise_weights(raw, VECTOR_SHARE_GATES[h]))
                     for pair, logits in enumerate(block_logits):
                         for i in range(GATES):
                             add_pass(logits[i][:, 0, :], gate_weights[q], i * BLOCK + PAIR * pair * P, q, all_passes)
@@ -274,7 +274,7 @@ def tile_vectormerge_pa_kernel(
                     for u in range(PAIR):
                         j = h * BLOCK_TILES + PAIR * pair + u
                         bg = [bg_sum[:, B_ROWS * i + j : B_ROWS * i + j + 1] for i in range(GATES)]
-                        l0 = merge.tile([P, ROWS], F32, tag="l0")
+                        l0 = merge.tile([P, ROWS], F32, tag="l0", bufs=2 * PAIR)
                         nc.scalar.activation(out=l0[:], in_=logits[0][:, u, :], func=ACT.Identity, bias=bg[0])
                         for i in (1, 2):
                             nc.vector.scalar_tensor_tensor(
@@ -309,8 +309,8 @@ def tile_vectormerge_pa_kernel(
                     for u in range(PAIR):
                         e = e_pairs[pair]
                         turn_sum(denom[:, m, u, :], [e[:, i, u, m * P : (m + 1) * P] for i in range(GATES)])
-                nc.scalar.activation(out=recip[:, pair], in_=denom[:], func=ACT.Ln, bias=zero[:])
-            nc.scalar.activation(out=recip[:], in_=recip[:], func=ACT.Exp, scale=-1.0)
+                nc.scalar.activation(out=recip[:, pair], in_=denom[:], func=ACT.Abs_reciprocal_sqrt, bias=zero[:])
+            nc.scalar.activation(out=recip[:], in_=recip[:], func=ACT.Square)
 
             for n in (2, 0, 1):
                 own_passes = [q for q in all_passes if PASSES[q][0] == n]

@@ -26,7 +26,7 @@ BLOCK_TILES = BLOCK // P
 COL_TILES = OUT // P
 PAIR = 2
 VECTOR_SHARE_GATES = (8, 9)
-VECTOR_SHARE_VALUES = 9
+VECTOR_SHARE_VALUES = 8
 BN_CHUNK = 512
 QUANTISE_WORDS = 1024
 
@@ -182,7 +182,10 @@ def tile_vectormerge_pa_kernel(
                                 scale=ln_cols[:, kt : kt + 1],
                             )
                     f_grouped = norm.tile([P, ROWS, PACK], BF16, tag="f_grouped", align_bytes=64)
-                    nc.vector.tensor_copy(out=f_grouped[:], in_=f_t[:].rearrange("p t r -> p r t"))
+                    nc.vector.tensor_copy(
+                        out=f_grouped[:].rearrange("p (c i) t -> p c t i", i=4),
+                        in_=f_t[:].rearrange("p t (c i) -> p c t i", i=4),
+                    )
                     nc.vector.quantize_mx(
                         out=f_codes[:, q, :].bitcast(FP8X4),
                         scales=f_scales[:, q, :],
@@ -310,7 +313,7 @@ def tile_vectormerge_pa_kernel(
                         e = e_pairs[pair]
                         turn_sum(denom[:, m, u, :], [e[:, i, u, m * P : (m + 1) * P] for i in range(GATES)])
                 nc.scalar.activation(out=recip[:, pair], in_=denom[:], func=ACT.Abs_reciprocal_sqrt, bias=zero[:])
-            nc.scalar.activation(out=recip[:], in_=recip[:], func=ACT.Square)
+                nc.scalar.activation(out=recip[:, pair], in_=recip[:, pair], func=ACT.Square)
 
             for n in (2, 0, 1):
                 own_passes = [q for q in all_passes if PASSES[q][0] == n]

from contextlib import ExitStack

import concourse.mybir as mybir
from concourse.masks import make_identity

F32 = mybir.dt.float32
BF16 = mybir.dt.bfloat16
U32 = mybir.dt.uint32
U8 = mybir.dt.uint8
FP8X4 = mybir.dt.float8_e4m3fn_x4
ACT = mybir.ActivationFunctionType
ALU = mybir.AluOpType

P = 128
PACK = 4
K_PASS = P * PACK
ROWS = 256
ROW_TILES = ROWS // P
OUT = 1024
GATES = 3
WIDTHS = (1024, 512, 2048)
EPS = 1e-5
BLOCK = 512
BLOCKS = OUT // BLOCK
BLOCK_TILES = BLOCK // P
COL_TILES = OUT // P
PAIR = 2
VECTOR_SHARE_GATES = (8, 9)
VECTOR_SHARE_VALUES = 8
BN_CHUNK = 512
QUANTISE_WORDS = 1024

STREAM_ORDER = (1, 0, 2)
PASSES = tuple((n, c) for n in STREAM_ORDER for c in range(WIDTHS[n] // K_PASS))
K_TILES = sum(WIDTHS) // P

FLOPS = 2 * ROWS * sum(WIDTHS) * (OUT + GATES * OUT)


def tile_vectormerge_pa_kernel(
    tc,
    x_a, ln_w_a, ln_b_a, W_a, b_a, Wg_a, bg_a,
    x_b, ln_w_b, ln_b_b, W_b, b_b, Wg_b, bg_b,
    x_c, ln_w_c, ln_b_c, W_c, b_c, Wg_c, bg_c,
    out,
):
    nc = tc.nc
    xs = (x_a, x_b, x_c)
    ln_ws = (ln_w_a, ln_w_b, ln_w_c)
    ln_bs = (ln_b_a, ln_b_b, ln_b_c)
    Ws = (W_a, W_b, W_c)
    bs = (b_a, b_b, b_c)
    Wgs = (Wg_a, Wg_b, Wg_c)
    bgs = (bg_a, bg_b, bg_c)
    B_ROWS = OUT // P
    BG_ROWS = GATES * B_ROWS

    with ExitStack() as stack:
        const = stack.enter_context(tc.tile_pool(name="const", bufs=1))
        raw_pool = stack.enter_context(tc.tile_pool(name="raw", bufs=4))
        grouped_pool = stack.enter_context(tc.tile_pool(name="grouped", bufs=3))
        codes_pool = stack.enter_context(tc.tile_pool(name="codes", bufs=len(PASSES) + 2))
        acc_pool = stack.enter_context(tc.psum_pool(name="acc", bufs=6))
        turn_pool = stack.enter_context(tc.psum_pool(name="turn", bufs=2))

        ident = const.tile([P, P], F32)
        make_identity(nc, ident[:])
        minus_ident = const.tile([P, P], F32)
        nc.vector.tensor_scalar_mul(out=minus_ident[:], in0=ident[:], scalar1=-1.0)
        x_sb = [const.tile([P, ROW_TILES, WIDTHS[n]], BF16, name="x%d" % n) for n in range(3)]

        def load_weights(pieces):
            width = sum(piece.shape[1] for piece in pieces)
            raw = raw_pool.tile([P, PACK, width], BF16, tag="raw")
            col0 = 0
            for piece in pieces:
                cols = piece.shape[1]
                nc.sync.dma_start(
                    out=raw[:, :, col0 : col0 + cols], in_=piece.rearrange("(t p) w -> p t w", p=P)
                )
                col0 += cols
            return raw

        def load_gates(h, q):
            n, c = PASSES[q]
            k_rows = slice(c * K_PASS, (c + 1) * K_PASS)
            return load_weights(
                [Wgs[n][k_rows, i * OUT + h * BLOCK : i * OUT + (h + 1) * BLOCK] for i in range(GATES)]
            )

        loaded = {}
        for n in STREAM_ORDER:
            if n == STREAM_ORDER[-1]:
                loaded[0, 0] = load_gates(0, 0)
            nc.sync.dma_start(out=x_sb[n][:], in_=xs[n].rearrange("(m p) d -> p m d", p=P))
        one = const.tile([P, 1], F32)
        nc.vector.memset(one[:], 1.0)
        table_loader = const.tile([P, 1], F32)
        nc.scalar.activation(out=table_loader[:], in_=one[:], func=ACT.Sqrt)
        f_codes = const.tile([P, len(PASSES), ROWS], U32, align_bytes=64)
        f_scales = const.tile([P, len(PASSES), ROWS], U8, align_bytes=64)

        ln_rows = const.tile([P, P], BF16)
        bias_rows = const.tile([P, P], BF16)
        nc.vector.memset(ln_rows[:], 0.0)
        nc.vector.memset(bias_rows[:], 0.0)
        k_tile0 = 0
        for n in STREAM_ORDER:
            k_tiles = WIDTHS[n] // P
            nc.scalar.dma_start(
                out=ln_rows[k_tile0 : k_tile0 + k_tiles, :],
                in_=ln_ws[n].rearrange("(r c) -> r c", c=P),
            )
            nc.scalar.dma_start(
                out=ln_rows[K_TILES + k_tile0 : K_TILES + k_tile0 + k_tiles, :],
                in_=ln_bs[n].rearrange("(r c) -> r c", c=P),
            )
            k_tile0 += k_tiles
        def to_columns(rows_bf16, name):
            rows_f32 = const.tile([P, P], F32, name=name + "_f32")
            nc.vector.tensor_copy(out=rows_f32[:], in_=rows_bf16[:])
            turned = turn_pool.tile([P, BLOCK], F32, tag="turn", name=name + "_ps")
            nc.tensor.transpose(turned[:, 0:P], rows_f32[:], ident[:])
            columns = const.tile([P, P], F32, name=name + "_cols")
            nc.vector.tensor_copy(out=columns[:], in_=turned[:, 0:P])
            return columns

        ln_cols = to_columns(ln_rows, "ln")

        with tc.tile_pool(name="norm", bufs=2) as norm:
            q = 0
            for n in STREAM_ORDER:
                d = WIDTHS[n]
                chunks = d // BN_CHUNK
                stats = norm.tile([P, ROW_TILES, chunks, 6], F32, name="stats%d" % n, bufs=1)
                mean_var = norm.tile([P, ROW_TILES, 2], F32, tag="mean_var", bufs=3)
                for m in range(ROW_TILES):
                    for j in range(chunks):
                        nc.vector.bn_stats(
                            out=stats[:, m, j, :],
                            in_=x_sb[n][:, m, j * BN_CHUNK : (j + 1) * BN_CHUNK],
                        )
                    nc.vector.bn_aggr(
                        out=mean_var[:, m, :], in_=stats[:, m, :, :].rearrange("p c s -> p (c s)")
                    )
                var_eps = norm.tile([P, ROW_TILES], F32, tag="var_eps", bufs=3)
                nc.vector.tensor_scalar_add(out=var_eps[:], in0=mean_var[:, :, 1], scalar1=EPS)
                minus_mean = norm.tile([P, ROW_TILES], F32, tag="minus_mean", bufs=3)
                nc.vector.tensor_scalar_mul(out=minus_mean[:], in0=mean_var[:, :, 0], scalar1=-1.0)
                sigma = norm.tile([P, ROW_TILES], F32, tag="sigma", bufs=3)
                nc.scalar.activation(out=sigma[:], in_=var_eps[:], func=ACT.Sqrt)
                rstd = norm.tile([P, ROW_TILES], F32, tag="rstd", bufs=3)
                nc.vector.reciprocal(out=rstd[:], in_=sigma[:])
                shift = norm.tile([P, ROW_TILES], F32, tag="shift", bufs=3)
                nc.vector.tensor_tensor(out=shift[:], in0=minus_mean[:], in1=rstd[:], op=ALU.mult)
                for c in range(d // K_PASS):
                    z = []
                    for m in range(ROW_TILES):
                        z_m = norm.tile([P, K_PASS], F32, tag="z", bufs=4, name="z%d" % m)
                        nc.scalar.activation(
                            out=z_m[:], in_=x_sb[n][:, m, c * K_PASS : (c + 1) * K_PASS],
                            func=ACT.Identity, bias=shift[:, m : m + 1], scale=rstd[:, m : m + 1],
                        )
                        z.append(z_m)
                    f_t = norm.tile([P, PACK, ROWS], BF16, tag="f_t")
                    for half in range(PACK // 2):
                        z_turned = turn_pool.tile([P, 2, ROWS], F32, tag="turn")
                        for u in range(2):
                            t = 2 * half + u
                            for m in range(ROW_TILES):
                                nc.tensor.transpose(
                                    z_turned[:, u, m * P : (m + 1) * P],
                                    z[m][:, t * P : (t + 1) * P],
                                    ident[:],
                                )
                        for u in range(2):
                            t = 2 * half + u
                            kt = PACK * q + t
                            nc.scalar.activation(
                                out=f_t[:, t, :], in_=z_turned[:, u, :], func=ACT.Relu,
                                bias=ln_cols[:, K_TILES + kt : K_TILES + kt + 1],
                                scale=ln_cols[:, kt : kt + 1],
                            )
                    f_grouped = norm.tile([P, ROWS, PACK], BF16, tag="f_grouped", align_bytes=64)
                    nc.vector.tensor_copy(
                        out=f_grouped[:].rearrange("p (c i) t -> p c t i", i=4),
                        in_=f_t[:].rearrange("p t (c i) -> p c t i", i=4),
                    )
                    nc.vector.quantize_mx(
                        out=f_codes[:, q, :].bitcast(FP8X4),
                        scales=f_scales[:, q, :],
                        in_=f_grouped[:].rearrange("p r t -> p (r t)"),
                    )
                    q += 1

        for n in range(3):
            nc.sync.dma_start(
                out=bias_rows[n * B_ROWS : (n + 1) * B_ROWS, :],
                in_=bs[n].rearrange("(r c) -> r c", c=P),
            )
            nc.sync.dma_start(
                out=bias_rows[3 * B_ROWS + n * BG_ROWS : 3 * B_ROWS + (n + 1) * BG_ROWS, :],
                in_=bgs[n].rearrange("(r c) -> r c", c=P),
            )

        bias_cols = to_columns(bias_rows, "bias")
        bg_sum = const.tile([P, BG_ROWS], F32)
        bg0 = 3 * B_ROWS
        nc.vector.tensor_tensor(
            out=bg_sum[:], in0=bias_cols[:, bg0 : bg0 + BG_ROWS],
            in1=bias_cols[:, bg0 + BG_ROWS : bg0 + 2 * BG_ROWS], op=ALU.add,
        )
        nc.vector.tensor_tensor(
            out=bg_sum[:], in0=bg_sum[:],
            in1=bias_cols[:, bg0 + 2 * BG_ROWS : bg0 + 3 * BG_ROWS], op=ALU.add,
        )

        def quantise_weights(raw, vector_share):
            width = raw.shape[2]
            grouped = grouped_pool.tile([P, width, PACK], BF16, tag="grouped", align_bytes=64)
            dst = grouped[:].rearrange("p (c i) t -> p c t i", i=4)
            src = raw[:].rearrange("p t (c i) -> p c t i", i=4)
            split = width * vector_share // 16 // 4
            nc.vector.tensor_copy(out=dst[:, 0:split], in_=src[:, 0:split])
            nc.scalar.copy(out=dst[:, split:], in_=src[:, split:])
            codes = codes_pool.tile([P, width], U32, tag="codes", align_bytes=64)
            scales = codes_pool.tile([P, width], U8, tag="scales", align_bytes=64)
            for col0 in range(0, width, QUANTISE_WORDS):
                cols = min(QUANTISE_WORDS, width - col0)
                nc.vector.quantize_mx(
                    out=codes[:, col0 : col0 + cols].bitcast(FP8X4),
                    scales=scales[:, col0 : col0 + cols],
                    in_=grouped[:, col0 : col0 + cols, :].rearrange("p w t -> p (w t)"),
                )
            return codes, scales

        def add_pass(acc, weights, col0, q, passes):
            codes, scales = weights
            nc.tensor.matmul_mx(
                out=acc,
                lhsT=codes[:, col0 : col0 + P].bitcast(FP8X4),
                lhsT_scale=scales[:, col0 : col0 + P],
                rhs=f_codes[:, q, :].bitcast(FP8X4),
                rhs_scale=f_scales[:, q, :],
                start=(q == passes[0]),
                stop=(q == passes[-1]),
            )

        def turn_sum(out, parts):
            for i, part in enumerate(parts):
                nc.tensor.matmul(
                    out=out, lhsT=part, rhs=ident[:], is_transpose=True,
                    start=(i == 0), stop=(i == len(parts) - 1),
                )

        all_passes = list(range(len(PASSES)))
        with tc.tile_pool(name="merge", bufs=2) as merge:
            e_pairs = []
            for h in range(BLOCKS):
                block_logits = [
                    [acc_pool.tile([P, PAIR, ROWS], F32, tag="acc", name="logits%d" % i) for i in range(GATES)]
                    for pair in range(BLOCK_TILES // PAIR)
                ]
                gate_weights = []
                for q in all_passes:
                    raw = loaded[h, q] if (h, q) in loaded else load_gates(h, q)
                    gate_weights.append(quantise_weights(raw, VECTOR_SHARE_GATES[h]))
                    for pair, logits in enumerate(block_logits):
                        for i in range(GATES):
                            add_pass(logits[i][:, 0, :], gate_weights[q], i * BLOCK + PAIR * pair * P, q, all_passes)
                for pair, logits in enumerate(block_logits):
                    for i in range(GATES):
                        for q in all_passes:
                            col0 = i * BLOCK + (PAIR * pair + 1) * P
                            add_pass(logits[i][:, 1, :], gate_weights[q], col0, q, all_passes)
                    diff = merge.tile([P, GATES - 1, PAIR, ROWS], F32, tag="diff")
                    for u in range(PAIR):
                        j = h * BLOCK_TILES + PAIR * pair + u
                        bg = [bg_sum[:, B_ROWS * i + j : B_ROWS * i + j + 1] for i in range(GATES)]
                        l0 = merge.tile([P, ROWS], F32, tag="l0", bufs=2 * PAIR)
                        nc.scalar.activation(out=l0[:], in_=logits[0][:, u, :], func=ACT.Identity, bias=bg[0])
                        for i in (1, 2):
                            nc.vector.scalar_tensor_tensor(
                                out=diff[:, i - 1, u, :], in0=logits[i][:, u, :], scalar=bg[i], in1=l0[:],
                                op0=ALU.add, op1=ALU.subtract,
                            )
                    top = merge.tile([P, PAIR, ROWS], F32, tag="top")
                    nc.vector.scalar_tensor_tensor(
                        out=top[:], in0=diff[:, 0], scalar=0.0, in1=diff[:, 1], op0=ALU.max, op1=ALU.max
                    )
                    e = merge.tile([P, GATES, PAIR, ROWS], F32, tag="e", bufs=COL_TILES // PAIR)
                    nc.scalar.activation(out=e[:, 0], in_=top[:], func=ACT.Exp, scale=-1.0)
                    for i in (1, 2):
                        for u in range(PAIR):
                            nc.tensor.matmul(
                                out=logits[i][:, u, :], lhsT=ident[:], rhs=diff[:, i - 1, u, :], start=True, stop=False
                            )
                            nc.tensor.matmul(
                                out=logits[i][:, u, :], lhsT=minus_ident[:], rhs=top[:, u, :], start=False, stop=True
                            )
                        nc.scalar.activation(out=e[:, i], in_=logits[i][:], func=ACT.Exp)
                    e_pairs.append(e)

            recip = merge.tile([P, COL_TILES // PAIR, ROW_TILES, PAIR, P], F32, tag="recip", bufs=1)
            zero = merge.tile([P, 1], F32, tag="zero", bufs=1)
            nc.vector.tensor_scalar(
                out=zero[:], in0=e_pairs[-1][:, GATES - 1, 0, 0:1], scalar1=0.0, scalar2=None, op0=ALU.mult
            )
            for pair in range(COL_TILES // PAIR):
                denom = turn_pool.tile([P, ROW_TILES, PAIR, P], F32, tag="turn")
                for m in range(ROW_TILES):
                    for u in range(PAIR):
                        e = e_pairs[pair]
                        turn_sum(denom[:, m, u, :], [e[:, i, u, m * P : (m + 1) * P] for i in range(GATES)])
                nc.scalar.activation(out=recip[:, pair], in_=denom[:], func=ACT.Abs_reciprocal_sqrt, bias=zero[:])
                nc.scalar.activation(out=recip[:, pair], in_=recip[:, pair], func=ACT.Square)

            for n in (2, 0, 1):
                own_passes = [q for q in all_passes if PASSES[q][0] == n]
                value_weights = {}
                for q in own_passes:
                    c = PASSES[q][1]
                    raw = load_weights([Ws[n][c * K_PASS : (c + 1) * K_PASS, :]])
                    value_weights[q] = quantise_weights(raw, VECTOR_SHARE_VALUES)
                for pair in range(COL_TILES // PAIR):
                    y = acc_pool.tile([P, PAIR, ROWS], F32, tag="acc")
                    for u in range(PAIR):
                        for q in own_passes:
                            add_pass(y[:, u, :], value_weights[q], (PAIR * pair + u) * P, q, own_passes)
                    for u in range(PAIR):
                        j = PAIR * pair + u
                        e_n = e_pairs[pair][:, n, u, :]
                        nc.vector.scalar_tensor_tensor(
                            out=e_n, in0=y[:, u, :], scalar=bias_cols[:, B_ROWS * n + j : B_ROWS * n + j + 1],
                            in1=e_n, op0=ALU.add, op1=ALU.mult,
                        )

            for pair in range(COL_TILES // PAIR):
                numer = acc_pool.tile([P, ROW_TILES, PAIR, P], F32, tag="acc")
                for m in range(ROW_TILES):
                    for u in range(PAIR):
                        e = e_pairs[pair]
                        turn_sum(numer[:, m, u, :], [e[:, n, u, m * P : (m + 1) * P] for n in range(3)])
                out_sb = merge.tile([P, ROW_TILES, PAIR, P], F32, tag="out_sb", bufs=COL_TILES // PAIR)
                nc.vector.tensor_tensor(out=out_sb[:], in0=numer[:], in1=recip[:, pair], op=ALU.mult)
                nc.sync.dma_start(
                    out=out[:, pair * PAIR * P : (pair + 1) * PAIR * P].rearrange("(m p) c -> p m c", p=P),
                    in_=out_sb[:].rearrange("p m u c -> p m (u c)"),
                )
